import numpy as np
import ml_dtypes


def mxq(x, axis, fmt="e4m3"):
    dtype, down = {"e4m3": (ml_dtypes.float8_e4m3fn, 7), "e5m2": (ml_dtypes.float8_e5m2, 14)}[fmt]
    v = np.moveaxis(np.asarray(x, np.float32).astype(ml_dtypes.bfloat16).astype(np.float64), axis, -1)
    blocks = v.reshape(v.shape[:-1] + (-1, 32))
    amax = np.abs(blocks).max(-1, keepdims=True)
    byte = np.maximum(np.where(amax > 0, np.frexp(amax)[1] - 1 + 127, 0) - down, 1)
    scale = np.exp2(byte - 127.0)
    codes = (blocks / scale).astype(np.float32).astype(dtype).astype(np.float64)
    return np.moveaxis((codes * scale).reshape(v.shape), -1, axis)


WIDE = False


def mx_kscale(k):
    if not WIDE:
        return np.ones(k)
    levels = np.array([10, -10, 5, -5, 0])
    a = np.random.permutation(np.resize(levels, k // 512 * 4)).reshape(k // 512, 4)
    idx = np.arange(k)
    return np.exp2(a[idx // 512, idx % 128 // 32])


BF16 = ml_dtypes.bfloat16


def bf(x):
    return np.asarray(x, np.float32).astype(BF16)


def f64(x):
    return np.asarray(x).astype(np.float64)


B, S, D, HQ, HK, HD = 4, 2048, 1024, 2, 2, 64
QD = HQ * HD
KD = HK * HD
E = QD + 2 * KD
EPS = 1e-6
ROPE_BASE = 10000.0
QK_RMS = 0.003


def rope_tables():
    inv_freq = 1.0 / ROPE_BASE ** (np.arange(0, HD, 2) / HD)
    freqs = np.outer(np.arange(S), inv_freq)
    emb = np.concatenate([freqs, freqs], axis=-1)
    return np.cos(emb), np.sin(emb)


def rms_norm(h, w):
    var = np.mean(np.square(h), axis=-1, keepdims=True)
    return h * (1.0 / np.sqrt(var + EPS)) * w


def rotate_half(h):
    h1, h2 = np.split(h, 2, axis=-1)
    return np.concatenate([-h2, h1], axis=-1)


def apply_rope(h, cos, sin):
    return h * cos[None, :, None, :] + rotate_half(h) * sin[None, :, None, :]


def setup_inputs():
    s = mx_kscale(D)
    cos, sin = rope_tables()
    row = np.concatenate([np.full(QD + KD, QK_RMS), np.ones(KD)])
    return {"x": bf(np.random.standard_normal((B, S, D)) * s),
            "pos_cos": bf(cos),
            "pos_sin": bf(sin),
            "w_qkv": bf(np.random.standard_normal((E, D)) * row[:, None] / np.sqrt(D) / s[None, :]),
            "q_norm_w": bf(1.0 + 0.1 * np.random.standard_normal(HD)),
            "k_norm_w": bf(1.0 + 0.1 * np.random.standard_normal(HD))}


def reference(x, pos_cos, pos_sin, w_qkv, q_norm_w, k_norm_w):
    xq = mxq(f64(x), 2, "e4m3")
    wt = f64(w_qkv).T
    q = (xq @ mxq(wt[:, :QD], 0, "e4m3")).reshape(B, S, HQ, HD)
    k = (xq @ mxq(wt[:, QD:QD + KD], 0, "e4m3")).reshape(B, S, HK, HD)
    v = (xq @ mxq(wt[:, QD + KD:], 0, "e4m3")).reshape(B, S, HK, HD)
    cos, sin = f64(pos_cos), f64(pos_sin)
    q = apply_rope(rms_norm(q, f64(q_norm_w)), cos, sin)
    k = apply_rope(rms_norm(k, f64(k_norm_w)), cos, sin)
    return q, k, v

@@ -1,0 +1,286 @@
+from contextlib import ExitStack
+
+import concourse.mybir as mybir
+from concourse.masks import make_identity
+
+F32 = mybir.dt.float32
+BF16 = mybir.dt.bfloat16
+U32 = mybir.dt.uint32
+U8 = mybir.dt.uint8
+FP8X4 = mybir.dt.float8_e4m3fn_x4
+ACT = mybir.ActivationFunctionType
+ALU = mybir.AluOpType
+
+P = 128
+BATCH = 4
+SEQ = 2048
+FEAT = 1024
+HEAD = 64
+HALF = HEAD // 2
+QK_HEADS = 4
+QK_COLS = QK_HEADS * HEAD
+OUT_COLS = 384
+V_COLS = OUT_COLS - QK_COLS
+EPS = 1e-6
+
+PACK = 4
+PASSES = FEAT // (P * PACK)
+PAIR = 2
+WORDS = FEAT // PAIR
+WORD_BLOCKS = WORDS // P
+
+TILES_PER_BATCH = SEQ // P
+BUNCH = 2
+CHUNK = 4
+BUNCHES_PER_CHUNK = CHUNK // BUNCH
+CHUNKS_PER_BATCH = TILES_PER_BATCH // CHUNK
+BUNCHES_PER_BATCH = TILES_PER_BATCH // BUNCH
+N_BUNCHES = BATCH * BUNCHES_PER_BATCH
+TURN_AHEAD = 3
+QUANT_AHEAD = 2
+X_BUFS = 10
+VECTOR_COPIES_ONE_IN = 6
+
+FLOPS = 2 * BATCH * SEQ * FEAT * OUT_COLS
+
+
+def tile_qwen3attention_pa_t_kernel(
+    tc, x, pos_cos, pos_sin, w_qkv, q_norm_w, k_norm_w, out_0, out_1, out_2
+):
+    nc = tc.nc
+    x_rows = x.rearrange("b (p t) k -> b p t k", t=TILES_PER_BATCH)
+    cos_rows = pos_cos.rearrange("(p t) d -> p t d", t=TILES_PER_BATCH)
+    sin_rows = pos_sin.rearrange("(p t) d -> p t d", t=TILES_PER_BATCH)
+    q_rows = out_0.rearrange("b (p t) h d -> b p t (h d)", t=TILES_PER_BATCH)
+    k_rows = out_1.rearrange("b (p t) h d -> b p t (h d)", t=TILES_PER_BATCH)
+    v_rows = out_2.rearrange("b (p t) h d -> b p t (h d)", t=TILES_PER_BATCH)
+
+    with ExitStack() as ctx:
+        const = ctx.enter_context(tc.tile_pool(name="const", bufs=1))
+        x_pool = ctx.enter_context(tc.tile_pool(name="x_pool", bufs=X_BUFS))
+        group_pool = ctx.enter_context(tc.tile_pool(name="group_pool", bufs=3))
+        code_pool = ctx.enter_context(tc.tile_pool(name="code_pool", bufs=QUANT_AHEAD + 2))
+        stat_pool = ctx.enter_context(tc.tile_pool(name="stat_pool", bufs=3))
+        prod_pool = ctx.enter_context(tc.tile_pool(name="prod_pool", bufs=3))
+        stage_pool = ctx.enter_context(tc.tile_pool(name="stage_pool", bufs=4))
+        psum_t = ctx.enter_context(tc.psum_pool(name="psum_t", bufs=3))
+        psum_qk = ctx.enter_context(tc.psum_pool(name="psum_qk", bufs=3))
+        psum_v = ctx.enter_context(tc.psum_pool(name="psum_v", bufs=2))
+        ctx.enter_context(tc.manual_schedule())
+
+        x_words = {}
+        grouped_of = {}
+        x_codes = {}
+        x_scales = {}
+        qk_sums = {}
+        rstd_of = {}
+        rope_of = {}
+        qk_stage = {}
+        v_stage = {}
+
+        def load_bunch(b):
+            if b >= N_BUNCHES:
+                return
+            t0 = (b % BUNCHES_PER_BATCH) * BUNCH
+            x_sb = x_pool.tile([P, BUNCH, FEAT], BF16, name="x_sb")
+            nc.sync.dma_start(
+                out=x_sb[:], in_=x_rows[b // BUNCHES_PER_BATCH, :, t0 : t0 + BUNCH, :]
+            )
+            x_words[b] = x_sb[:].bitcast(F32)
+
+        def turn_rows(words):
+            turned = psum_t.tile([P, WORD_BLOCKS, P], F32, name="turned")
+            for j in range(WORD_BLOCKS):
+                nc.tensor.transpose(turned[:, j, :], words[:, j * P : (j + 1) * P], ident[:])
+            return turned[:].rearrange("p (g u) r -> p g r u", u=PAIR)
+
+        def turn_and_regroup(b):
+            if b >= N_BUNCHES:
+                return
+            grouped = group_pool.tile(
+                [P, BUNCH, PASSES, P * PACK], BF16, name="grouped", align_bytes=64
+            )
+            grouped_words = grouped[:].bitcast(F32).rearrange(
+                "p i g (r u) -> p i g r u", u=PAIR
+            )
+            for i in range(BUNCH):
+                turned = turn_rows(x_words[b][:, i, :])
+                if (b * BUNCH + i) % VECTOR_COPIES_ONE_IN == VECTOR_COPIES_ONE_IN - 1:
+                    nc.vector.tensor_copy(out=grouped_words[:, i], in_=turned)
+                else:
+                    nc.scalar.copy(out=grouped_words[:, i], in_=turned)
+            grouped_of[b] = grouped
+            load_bunch(b + X_BUFS)
+
+        def quantise(b):
+            if b >= N_BUNCHES:
+                return
+            codes = code_pool.tile([P, BUNCH, PASSES, P], U32, name="codes", align_bytes=64)
+            scales = code_pool.tile([P, BUNCH, PASSES, P], U8, name="scales", align_bytes=64)
+            nc.vector.quantize_mx(
+                out=codes[:].rearrange("p i g r -> p (i g r)").bitcast(FP8X4),
+                scales=scales[:].rearrange("p i g r -> p (i g r)"),
+                in_=grouped_of[b][:].rearrange("p i g c -> p (i g c)"),
+            )
+            x_codes[b] = codes
+            x_scales[b] = scales
+
+        def project(b):
+            qk_ps = psum_qk.tile([P, BUNCH, QK_COLS], F32, name="qk_ps")
+            v_ps = psum_v.tile([P, BUNCH, V_COLS], F32, name="v_ps")
+            for i in range(BUNCH):
+                for g in range(PASSES):
+                    for acc, lo, hi in ((qk_ps, 0, QK_COLS), (v_ps, QK_COLS, OUT_COLS)):
+                        nc.tensor.matmul_mx(
+                            out=acc[:, i, :],
+                            lhsT=x_codes[b][:, i, g, :].bitcast(FP8X4),
+                            lhsT_scale=x_scales[b][:, i, g, :],
+                            rhs=w_codes[:, g, lo:hi].bitcast(FP8X4),
+                            rhs_scale=w_scales[:, g, lo:hi],
+                            start=(g == 0),
+                            stop=(g == PASSES - 1),
+                        )
+            qk_sums[b] = qk_ps[:].rearrange("p i (h d) -> p (i h) d", d=HEAD)
+            return v_ps
+
+        def norm_factors(b, v_ps):
+            c = b // BUNCHES_PER_CHUNK
+            i0 = (b % BUNCHES_PER_CHUNK) * BUNCH
+            n_heads = BUNCH * QK_HEADS
+            squares = stat_pool.tile([P, n_heads, HEAD], F32, name="squares")
+            mean_sq = stat_pool.tile([P, n_heads], F32, name="mean_sq")
+            for n in range(n_heads):
+                nc.scalar.activation(
+                    out=squares[:, n, :],
+                    in_=qk_sums[b][:, n, :],
+                    func=ACT.Square,
+                    scale=1.0 / 8.0,
+                    accum_out=mean_sq[:, n : n + 1],
+                )
+            if i0 == 0:
+                v_stage[c] = stage_pool.tile([P, CHUNK, V_COLS], F32, name="v_out")
+            nc.scalar.copy(out=v_stage[c][:, i0 : i0 + BUNCH, :], in_=v_ps[:])
+            std = stat_pool.tile([P, n_heads], F32, name="std")
+            nc.scalar.activation(
+                out=std[:], in_=mean_sq[:], func=ACT.Sqrt, bias=eps_col[:], scale=1.0
+            )
+            rstd = stat_pool.tile([P, n_heads], F32, name="rstd")
+            nc.vector.reciprocal(rstd[:], std[:])
+            rstd_of[b] = rstd
+
+        def norm_and_rope(b):
+            c = b // BUNCHES_PER_CHUNK
+            i0 = (b % BUNCHES_PER_CHUNK) * BUNCH
+            rope = rope_of[c % CHUNKS_PER_BATCH]
+            prods = prod_pool.tile([P, 2, BUNCH, 2, 2, HEAD], F32, name="prods")
+            for i in range(BUNCH):
+                for qk in range(2):
+                    for h in range(2):
+                        n = i * QK_HEADS + qk * 2 + h
+                        nc.vector.scalar_tensor_tensor(
+                            out=prods[:, qk, i, h, :, :],
+                            in0=qk_sums[b][:, n, :].unsqueeze(1).broadcast_to([P, 2, HEAD]),
+                            scalar=rstd_of[b][:, n : n + 1],
+                            in1=rope[:, i0 + i, qk, :, :],
+                            op0=ALU.mult,
+                            op1=ALU.mult,
+                        )
+            if i0 == 0:
+                qk_stage[c] = stage_pool.tile([P, 2, CHUNK, 2 * HEAD], F32, name="qk_out")
+            done = qk_stage[c][:, :, i0 : i0 + BUNCH, :].rearrange(
+                "p q i (h d) -> p q (i h) d", d=HEAD
+            )
+            terms = prods[:].rearrange("p q i h a d -> p q (i h) a d")
+            nc.gpsimd.tensor_tensor(
+                out=done[:, :, :, 0:HALF],
+                in0=terms[:, :, :, 0, 0:HALF],
+                in1=terms[:, :, :, 1, HALF:HEAD],
+                op=ALU.subtract,
+            )
+            nc.gpsimd.tensor_tensor(
+                out=done[:, :, :, HALF:HEAD],
+                in0=terms[:, :, :, 0, HALF:HEAD],
+                in1=terms[:, :, :, 1, 0:HALF],
+                op=ALU.add,
+            )
+
+        def store_chunk(c):
+            batch = c // CHUNKS_PER_BATCH
+            t0 = (c % CHUNKS_PER_BATCH) * CHUNK
+            nc.sync.dma_start(out=v_rows[batch, :, t0 : t0 + CHUNK, :], in_=v_stage[c][:])
+            nc.sync.dma_start(out=q_rows[batch, :, t0 : t0 + CHUNK, :], in_=qk_stage[c][:, 0])
+            nc.sync.dma_start(out=k_rows[batch, :, t0 : t0 + CHUNK, :], in_=qk_stage[c][:, 1])
+
+        w_sb = const.tile([P, OUT_COLS // P, FEAT], BF16, name="w_sb")
+        gains = const.tile([P, 2, HEAD], BF16, name="gains")
+        cos_sb = const.tile([P, TILES_PER_BATCH, HEAD], BF16, name="cos_sb")
+        sin_sb = const.tile([P, TILES_PER_BATCH, HEAD], BF16, name="sin_sb")
+        load_bunch(0)
+        nc.sync.dma_start(out=w_sb[:], in_=w_qkv.rearrange("(c p) k -> p c k", p=P))
+        load_bunch(1)
+        nc.sync.dma_start(out=gains[:, 0, :], in_=q_norm_w.partition_broadcast(P))
+        nc.sync.dma_start(out=gains[:, 1, :], in_=k_norm_w.partition_broadcast(P))
+        nc.sync.dma_start(out=cos_sb[:], in_=cos_rows)
+        nc.sync.dma_start(out=sin_sb[:], in_=sin_rows)
+        for b in range(2, X_BUFS):
+            load_bunch(b)
+
+        ident = const.tile([P, P], F32, name="ident")
+        make_identity(nc, ident[:])
+        eps_col = const.tile([P, 1], F32, name="eps_col")
+        nc.vector.memset(eps_col[:], EPS)
+        warm = const.tile([P, 1], F32, name="warm")
+        nc.scalar.activation(out=warm[:], in_=eps_col[:], func=ACT.Sqrt)
+
+        for c in range(CHUNKS_PER_BATCH):
+            tiles = slice(c * CHUNK, (c + 1) * CHUNK)
+            rope_c = const.tile([P, CHUNK, 2, 2, HEAD], F32, name="rope%d" % c)
+            nc.gpsimd.tensor_tensor(
+                out=rope_c[:, :, :, 0, :],
+                in0=cos_sb[:, tiles, :].unsqueeze(2).broadcast_to([P, CHUNK, 2, HEAD]),
+                in1=gains[:].unsqueeze(1).broadcast_to([P, CHUNK, 2, HEAD]),
+                op=ALU.mult,
+            )
+            for mine, other in ((0, HALF), (HALF, 0)):
+                nc.gpsimd.tensor_tensor(
+                    out=rope_c[:, :, :, 1, mine : mine + HALF],
+                    in0=sin_sb[:, tiles, other : other + HALF]
+                    .unsqueeze(2)
+                    .broadcast_to([P, CHUNK, 2, HALF]),
+                    in1=gains[:, :, mine : mine + HALF]
+                    .unsqueeze(1)
+                    .broadcast_to([P, CHUNK, 2, HALF]),
+                    op=ALU.mult,
+                )
+            rope_of[c] = rope_c
+
+        turn_and_regroup(0)
+
+        w_words = w_sb[:].bitcast(F32)
+        w_grouped = const.tile([P, PASSES, OUT_COLS * PACK], BF16, name="w_grouped", align_bytes=64)
+        w_grouped_words = w_grouped[:].bitcast(F32).rearrange("p g (e u) -> p g e u", u=PAIR)
+        w_codes = const.tile([P, PASSES, OUT_COLS], U32, name="w_codes", align_bytes=64)
+        w_scales = const.tile([P, PASSES, OUT_COLS], U8, name="w_scales", align_bytes=64)
+        for blk in range(OUT_COLS // P):
+            turned_w = turn_rows(w_words[:, blk, :])
+            nc.scalar.copy(out=w_grouped_words[:, :, blk * P : (blk + 1) * P, :], in_=turned_w)
+        for g in range(PASSES):
+            for lo, hi in ((0, QK_COLS), (QK_COLS, OUT_COLS)):
+                nc.vector.quantize_mx(
+                    out=w_codes[:, g, lo:hi].bitcast(FP8X4),
+                    scales=w_scales[:, g, lo:hi],
+                    in_=w_grouped[:, g, lo * PACK : hi * PACK],
+                )
+
+        for b in range(1, TURN_AHEAD):
+            turn_and_regroup(b)
+        for b in range(QUANT_AHEAD):
+            quantise(b)
+        for b in range(N_BUNCHES):
+            turn_and_regroup(b + TURN_AHEAD)
+            v_sums = project(b)
+            norm_factors(b, v_sums)
+            quantise(b + QUANT_AHEAD)
+            norm_and_rope(b)
+            if b % BUNCHES_PER_CHUNK == BUNCHES_PER_CHUNK - 1:
+                store_chunk(b // BUNCHES_PER_CHUNK)

@@ -36,10 +36,10 @@ BUNCHES_PER_CHUNK = CHUNK // BUNCH
 CHUNKS_PER_BATCH = TILES_PER_BATCH // CHUNK
 BUNCHES_PER_BATCH = TILES_PER_BATCH // BUNCH
 N_BUNCHES = BATCH * BUNCHES_PER_BATCH
-TURN_AHEAD = 3
-QUANT_AHEAD = 2
-X_BUFS = 10
-VECTOR_COPIES_ONE_IN = 6
+N_CHUNKS = BATCH * CHUNKS_PER_BATCH
+TURN_AHEAD = 2 * BUNCHES_PER_CHUNK
+X_BUFS = 12
+assert BUNCH == 2
 
 FLOPS = 2 * BATCH * SEQ * FEAT * OUT_COLS
 
@@ -59,7 +59,7 @@ def tile_qwen3attention_pa_t_kernel(
         const = ctx.enter_context(tc.tile_pool(name="const", bufs=1))
         x_pool = ctx.enter_context(tc.tile_pool(name="x_pool", bufs=X_BUFS))
         group_pool = ctx.enter_context(tc.tile_pool(name="group_pool", bufs=3))
-        code_pool = ctx.enter_context(tc.tile_pool(name="code_pool", bufs=QUANT_AHEAD + 2))
+        code_pool = ctx.enter_context(tc.tile_pool(name="code_pool", bufs=3))
         stat_pool = ctx.enter_context(tc.tile_pool(name="stat_pool", bufs=3))
         prod_pool = ctx.enter_context(tc.tile_pool(name="prod_pool", bufs=3))
         stage_pool = ctx.enter_context(tc.tile_pool(name="stage_pool", bufs=4))
@@ -69,13 +69,17 @@ def tile_qwen3attention_pa_t_kernel(
         ctx.enter_context(tc.manual_schedule())
 
         x_words = {}
+        turned_of = {}
         grouped_of = {}
         x_codes = {}
         x_scales = {}
         qk_sums = {}
+        v_sums = {}
+        mean_sq_of = {}
+        std_of = {}
         rstd_of = {}
         rope_of = {}
-        qk_stage = {}
+        prods_of = {}
         v_stage = {}
 
         def load_bunch(b):
@@ -94,38 +98,42 @@ def tile_qwen3attention_pa_t_kernel(
                 nc.tensor.transpose(turned[:, j, :], words[:, j * P : (j + 1) * P], ident[:])
             return turned[:].rearrange("p (g u) r -> p g r u", u=PAIR)
 
-        def turn_and_regroup(b):
+        def turn_bunch(b):
             if b >= N_BUNCHES:
                 return
-            grouped = group_pool.tile(
-                [P, BUNCH, PASSES, P * PACK], BF16, name="grouped", align_bytes=64
-            )
-            grouped_words = grouped[:].bitcast(F32).rearrange(
-                "p i g (r u) -> p i g r u", u=PAIR
-            )
             for i in range(BUNCH):
-                turned = turn_rows(x_words[b][:, i, :])
-                if (b * BUNCH + i) % VECTOR_COPIES_ONE_IN == VECTOR_COPIES_ONE_IN - 1:
-                    nc.vector.tensor_copy(out=grouped_words[:, i], in_=turned)
-                else:
-                    nc.scalar.copy(out=grouped_words[:, i], in_=turned)
-            grouped_of[b] = grouped
+                turned_of[b * BUNCH + i] = turn_rows(x_words[b][:, i, :])
             load_bunch(b + X_BUFS)
 
-        def quantise(b):
-            if b >= N_BUNCHES:
+        def regroup_tile(tile):
+            if tile >= N_BUNCHES * BUNCH:
                 return
-            codes = code_pool.tile([P, BUNCH, PASSES, P], U32, name="codes", align_bytes=64)
-            scales = code_pool.tile([P, BUNCH, PASSES, P], U8, name="scales", align_bytes=64)
+            c = tile // CHUNK
+            if tile % CHUNK == 0:
+                grouped_of[c] = group_pool.tile(
+                    [P, CHUNK, PASSES, P * PACK], BF16, name="grouped", align_bytes=64
+                )
+            grouped_words = grouped_of[c][:].bitcast(F32).rearrange(
+                "p i g (r u) -> p i g r u", u=PAIR
+            )
+            nc.scalar.copy(out=grouped_words[:, tile % CHUNK], in_=turned_of[tile])
+
+        def quantise_chunk(c):
+            if c >= N_CHUNKS:
+                return
+            codes = code_pool.tile([P, CHUNK, PASSES, P], U32, name="codes", align_bytes=64)
+            scales = code_pool.tile([P, CHUNK, PASSES, P], U8, name="scales", align_bytes=64)
             nc.vector.quantize_mx(
                 out=codes[:].rearrange("p i g r -> p (i g r)").bitcast(FP8X4),
                 scales=scales[:].rearrange("p i g r -> p (i g r)"),
-                in_=grouped_of[b][:].rearrange("p i g c -> p (i g c)"),
+                in_=grouped_of[c][:].rearrange("p i g c -> p (i g c)"),
             )
-            x_codes[b] = codes
-            x_scales[b] = scales
+            x_codes[c] = codes
+            x_scales[c] = scales
 
         def project(b):
+            c = b // BUNCHES_PER_CHUNK
+            i0 = (b % BUNCHES_PER_CHUNK) * BUNCH
             qk_ps = psum_qk.tile([P, BUNCH, QK_COLS], F32, name="qk_ps")
             v_ps = psum_v.tile([P, BUNCH, V_COLS], F32, name="v_ps")
             for i in range(BUNCH):
@@ -133,19 +141,17 @@ def tile_qwen3attention_pa_t_kernel(
                     for acc, lo, hi in ((qk_ps, 0, QK_COLS), (v_ps, QK_COLS, OUT_COLS)):
                         nc.tensor.matmul_mx(
                             out=acc[:, i, :],
-                            lhsT=x_codes[b][:, i, g, :].bitcast(FP8X4),
-                            lhsT_scale=x_scales[b][:, i, g, :],
+                            lhsT=x_codes[c][:, i0 + i, g, :].bitcast(FP8X4),
+                            lhsT_scale=x_scales[c][:, i0 + i, g, :],
                             rhs=w_codes[:, g, lo:hi].bitcast(FP8X4),
                             rhs_scale=w_scales[:, g, lo:hi],
                             start=(g == 0),
                             stop=(g == PASSES - 1),
                         )
             qk_sums[b] = qk_ps[:].rearrange("p i (h d) -> p (i h) d", d=HEAD)
-            return v_ps
+            v_sums[b] = v_ps
 
-        def norm_factors(b, v_ps):
-            c = b // BUNCHES_PER_CHUNK
-            i0 = (b % BUNCHES_PER_CHUNK) * BUNCH
+        def mean_squares(b):
             n_heads = BUNCH * QK_HEADS
             squares = stat_pool.tile([P, n_heads, HEAD], F32, name="squares")
             mean_sq = stat_pool.tile([P, n_heads], F32, name="mean_sq")
@@ -157,59 +163,67 @@ def tile_qwen3attention_pa_t_kernel(
                     scale=1.0 / 8.0,
                     accum_out=mean_sq[:, n : n + 1],
                 )
-            if i0 == 0:
-                v_stage[c] = stage_pool.tile([P, CHUNK, V_COLS], F32, name="v_out")
-            nc.scalar.copy(out=v_stage[c][:, i0 : i0 + BUNCH, :], in_=v_ps[:])
-            std = stat_pool.tile([P, n_heads], F32, name="std")
+            mean_sq_of[b] = mean_sq
+
+        def roots(b):
+            std = stat_pool.tile([P, BUNCH * QK_HEADS], F32, name="std")
             nc.scalar.activation(
-                out=std[:], in_=mean_sq[:], func=ACT.Sqrt, bias=eps_col[:], scale=1.0
+                out=std[:], in_=mean_sq_of[b][:], func=ACT.Sqrt, bias=eps_col[:], scale=1.0
             )
-            rstd = stat_pool.tile([P, n_heads], F32, name="rstd")
-            nc.vector.reciprocal(rstd[:], std[:])
+            std_of[b] = std
+
+        def reciprocals(b):
+            rstd = stat_pool.tile([P, BUNCH * QK_HEADS], F32, name="rstd")
+            nc.vector.reciprocal(rstd[:], std_of[b][:])
             rstd_of[b] = rstd
 
-        def norm_and_rope(b):
+        def copy_v(b):
+            c = b // BUNCHES_PER_CHUNK
+            i0 = (b % BUNCHES_PER_CHUNK) * BUNCH
+            if i0 == 0:
+                v_stage[c] = stage_pool.tile([P, CHUNK, V_COLS], F32, name="v_out")
+            nc.vector.tensor_copy(out=v_stage[c][:, i0 : i0 + BUNCH, :], in_=v_sums[b][:])
+
+        def rope_products(b):
             c = b // BUNCHES_PER_CHUNK
             i0 = (b % BUNCHES_PER_CHUNK) * BUNCH
             rope = rope_of[c % CHUNKS_PER_BATCH]
-            prods = prod_pool.tile([P, 2, BUNCH, 2, 2, HEAD], F32, name="prods")
+            if i0 == 0:
+                prods_of[c] = prod_pool.tile([P, 2, CHUNK, 2, 2, HEAD], F32, name="prods")
             for i in range(BUNCH):
                 for qk in range(2):
                     for h in range(2):
                         n = i * QK_HEADS + qk * 2 + h
                         nc.vector.scalar_tensor_tensor(
-                            out=prods[:, qk, i, h, :, :],
+                            out=prods_of[c][:, qk, i0 + i, h, :, :],
                             in0=qk_sums[b][:, n, :].unsqueeze(1).broadcast_to([P, 2, HEAD]),
                             scalar=rstd_of[b][:, n : n + 1],
                             in1=rope[:, i0 + i, qk, :, :],
                             op0=ALU.mult,
                             op1=ALU.mult,
                         )
-            if i0 == 0:
-                qk_stage[c] = stage_pool.tile([P, 2, CHUNK, 2 * HEAD], F32, name="qk_out")
-            done = qk_stage[c][:, :, i0 : i0 + BUNCH, :].rearrange(
-                "p q i (h d) -> p q (i h) d", d=HEAD
-            )
-            terms = prods[:].rearrange("p q i h a d -> p q (i h) a d")
+
+        def add_and_store(c):
+            qk_out = stage_pool.tile([P, 2, CHUNK, 2 * HEAD], F32, name="qk_out")
+            done = qk_out[:].rearrange("p q i (h d) -> p (q i h) d", d=HEAD)
+            terms = prods_of[c][:].rearrange("p q i h a d -> p (q i h) a d")
             nc.gpsimd.tensor_tensor(
-                out=done[:, :, :, 0:HALF],
-                in0=terms[:, :, :, 0, 0:HALF],
-                in1=terms[:, :, :, 1, HALF:HEAD],
+                out=done[:, :, 0:HALF],
+                in0=terms[:, :, 0, 0:HALF],
+                in1=terms[:, :, 1, HALF:HEAD],
                 op=ALU.subtract,
             )
             nc.gpsimd.tensor_tensor(
-                out=done[:, :, :, HALF:HEAD],
-                in0=terms[:, :, :, 0, HALF:HEAD],
-                in1=terms[:, :, :, 1, 0:HALF],
+                out=done[:, :, HALF:HEAD],
+                in0=terms[:, :, 0, HALF:HEAD],
+                in1=terms[:, :, 1, 0:HALF],
                 op=ALU.add,
             )
-
-        def store_chunk(c):
             batch = c // CHUNKS_PER_BATCH
             t0 = (c % CHUNKS_PER_BATCH) * CHUNK
             nc.sync.dma_start(out=v_rows[batch, :, t0 : t0 + CHUNK, :], in_=v_stage[c][:])
-            nc.sync.dma_start(out=q_rows[batch, :, t0 : t0 + CHUNK, :], in_=qk_stage[c][:, 0])
-            nc.sync.dma_start(out=k_rows[batch, :, t0 : t0 + CHUNK, :], in_=qk_stage[c][:, 1])
+            nc.sync.dma_start(out=q_rows[batch, :, t0 : t0 + CHUNK, :], in_=qk_out[:, 0])
+            nc.sync.dma_start(out=k_rows[batch, :, t0 : t0 + CHUNK, :], in_=qk_out[:, 1])
 
         w_sb = const.tile([P, OUT_COLS // P, FEAT], BF16, name="w_sb")
         gains = const.tile([P, 2, HEAD], BF16, name="gains")
@@ -217,12 +231,11 @@ def tile_qwen3attention_pa_t_kernel(
         sin_sb = const.tile([P, TILES_PER_BATCH, HEAD], BF16, name="sin_sb")
         load_bunch(0)
         nc.sync.dma_start(out=w_sb[:], in_=w_qkv.rearrange("(c p) k -> p c k", p=P))
-        load_bunch(1)
         nc.sync.dma_start(out=gains[:, 0, :], in_=q_norm_w.partition_broadcast(P))
         nc.sync.dma_start(out=gains[:, 1, :], in_=k_norm_w.partition_broadcast(P))
         nc.sync.dma_start(out=cos_sb[:], in_=cos_rows)
         nc.sync.dma_start(out=sin_sb[:], in_=sin_rows)
-        for b in range(2, X_BUFS):
+        for b in range(1, X_BUFS):
             load_bunch(b)
 
         ident = const.tile([P, P], F32, name="ident")
@@ -233,16 +246,17 @@ def tile_qwen3attention_pa_t_kernel(
         nc.scalar.activation(out=warm[:], in_=eps_col[:], func=ACT.Sqrt)
 
         for c in range(CHUNKS_PER_BATCH):
+            maker = nc.vector if c == 0 else nc.gpsimd
             tiles = slice(c * CHUNK, (c + 1) * CHUNK)
             rope_c = const.tile([P, CHUNK, 2, 2, HEAD], F32, name="rope%d" % c)
-            nc.gpsimd.tensor_tensor(
+            maker.tensor_tensor(
                 out=rope_c[:, :, :, 0, :],
                 in0=cos_sb[:, tiles, :].unsqueeze(2).broadcast_to([P, CHUNK, 2, HEAD]),
                 in1=gains[:].unsqueeze(1).broadcast_to([P, CHUNK, 2, HEAD]),
                 op=ALU.mult,
             )
             for mine, other in ((0, HALF), (HALF, 0)):
-                nc.gpsimd.tensor_tensor(
+                maker.tensor_tensor(
                     out=rope_c[:, :, :, 1, mine : mine + HALF],
                     in0=sin_sb[:, tiles, other : other + HALF]
                     .unsqueeze(2)
@@ -254,7 +268,9 @@ def tile_qwen3attention_pa_t_kernel(
                 )
             rope_of[c] = rope_c
 
-        turn_and_regroup(0)
+        turn_bunch(0)
+        for i in range(BUNCH):
+            regroup_tile(i)
 
         w_words = w_sb[:].bitcast(F32)
         w_grouped = const.tile([P, PASSES, OUT_COLS * PACK], BF16, name="w_grouped", align_bytes=64)
@@ -273,14 +289,23 @@ def tile_qwen3attention_pa_t_kernel(
                 )
 
         for b in range(1, TURN_AHEAD):
-            turn_and_regroup(b)
-        for b in range(QUANT_AHEAD):
-            quantise(b)
+            turn_bunch(b)
+            for i in range(BUNCH):
+                regroup_tile(b * BUNCH + i)
+        quantise_chunk(0)
         for b in range(N_BUNCHES):
-            turn_and_regroup(b + TURN_AHEAD)
-            v_sums = project(b)
-            norm_factors(b, v_sums)
-            quantise(b + QUANT_AHEAD)
-            norm_and_rope(b)
+            ahead = b + TURN_AHEAD
+            c = b // BUNCHES_PER_CHUNK
+            turn_bunch(ahead)
+            project(b)
+            regroup_tile(ahead * BUNCH)
+            mean_squares(b)
+            regroup_tile(ahead * BUNCH + 1)
+            roots(b)
+            if b % BUNCHES_PER_CHUNK == 0:
+                quantise_chunk(c + 1)
+            reciprocals(b)
+            copy_v(b)
+            rope_products(b)
             if b % BUNCHES_PER_CHUNK == BUNCHES_PER_CHUNK - 1:
-                store_chunk(b // BUNCHES_PER_CHUNK)
+                add_and_store(c)

@@ -36,8 +36,8 @@ BUNCHES_PER_CHUNK = CHUNK // BUNCH
 CHUNKS_PER_BATCH = TILES_PER_BATCH // CHUNK
 BUNCHES_PER_BATCH = TILES_PER_BATCH // BUNCH
 N_BUNCHES = BATCH * BUNCHES_PER_BATCH
-N_CHUNKS = BATCH * CHUNKS_PER_BATCH
-TURN_AHEAD = 2 * BUNCHES_PER_CHUNK
+TURN_AHEAD = 3
+QUANT_AHEAD = 2
 X_BUFS = 12
 assert BUNCH == 2
 
@@ -59,7 +59,7 @@ def tile_qwen3attention_pa_t_kernel(
         const = ctx.enter_context(tc.tile_pool(name="const", bufs=1))
         x_pool = ctx.enter_context(tc.tile_pool(name="x_pool", bufs=X_BUFS))
         group_pool = ctx.enter_context(tc.tile_pool(name="group_pool", bufs=3))
-        code_pool = ctx.enter_context(tc.tile_pool(name="code_pool", bufs=3))
+        code_pool = ctx.enter_context(tc.tile_pool(name="code_pool", bufs=QUANT_AHEAD + 2))
         stat_pool = ctx.enter_context(tc.tile_pool(name="stat_pool", bufs=3))
         prod_pool = ctx.enter_context(tc.tile_pool(name="prod_pool", bufs=3))
         stage_pool = ctx.enter_context(tc.tile_pool(name="stage_pool", bufs=4))
@@ -76,10 +76,10 @@ def tile_qwen3attention_pa_t_kernel(
         qk_sums = {}
         v_sums = {}
         mean_sq_of = {}
-        std_of = {}
         rstd_of = {}
         rope_of = {}
         prods_of = {}
+        qk_stage = {}
         v_stage = {}
 
         def load_bunch(b):
@@ -108,32 +108,30 @@ def tile_qwen3attention_pa_t_kernel(
         def regroup_tile(tile):
             if tile >= N_BUNCHES * BUNCH:
                 return
-            c = tile // CHUNK
-            if tile % CHUNK == 0:
-                grouped_of[c] = group_pool.tile(
-                    [P, CHUNK, PASSES, P * PACK], BF16, name="grouped", align_bytes=64
+            b = tile // BUNCH
+            if tile % BUNCH == 0:
+                grouped_of[b] = group_pool.tile(
+                    [P, BUNCH, PASSES, P * PACK], BF16, name="grouped", align_bytes=64
                 )
-            grouped_words = grouped_of[c][:].bitcast(F32).rearrange(
+            grouped_words = grouped_of[b][:].bitcast(F32).rearrange(
                 "p i g (r u) -> p i g r u", u=PAIR
             )
-            nc.scalar.copy(out=grouped_words[:, tile % CHUNK], in_=turned_of[tile])
+            nc.scalar.copy(out=grouped_words[:, tile % BUNCH], in_=turned_of[tile])
 
-        def quantise_chunk(c):
-            if c >= N_CHUNKS:
+        def quantise(b):
+            if b >= N_BUNCHES:
                 return
-            codes = code_pool.tile([P, CHUNK, PASSES, P], U32, name="codes", align_bytes=64)
-            scales = code_pool.tile([P, CHUNK, PASSES, P], U8, name="scales", align_bytes=64)
+            codes = code_pool.tile([P, BUNCH, PASSES, P], U32, name="codes", align_bytes=64)
+            scales = code_pool.tile([P, BUNCH, PASSES, P], U8, name="scales", align_bytes=64)
             nc.vector.quantize_mx(
                 out=codes[:].rearrange("p i g r -> p (i g r)").bitcast(FP8X4),
                 scales=scales[:].rearrange("p i g r -> p (i g r)"),
-                in_=grouped_of[c][:].rearrange("p i g c -> p (i g c)"),
+                in_=grouped_of[b][:].rearrange("p i g c -> p (i g c)"),
             )
-            x_codes[c] = codes
-            x_scales[c] = scales
+            x_codes[b] = codes
+            x_scales[b] = scales
 
         def project(b):
-            c = b // BUNCHES_PER_CHUNK
-            i0 = (b % BUNCHES_PER_CHUNK) * BUNCH
             qk_ps = psum_qk.tile([P, BUNCH, QK_COLS], F32, name="qk_ps")
             v_ps = psum_v.tile([P, BUNCH, V_COLS], F32, name="v_ps")
             for i in range(BUNCH):
@@ -141,8 +139,8 @@ def tile_qwen3attention_pa_t_kernel(
                     for acc, lo, hi in ((qk_ps, 0, QK_COLS), (v_ps, QK_COLS, OUT_COLS)):
                         nc.tensor.matmul_mx(
                             out=acc[:, i, :],
-                            lhsT=x_codes[c][:, i0 + i, g, :].bitcast(FP8X4),
-                            lhsT_scale=x_scales[c][:, i0 + i, g, :],
+                            lhsT=x_codes[b][:, i, g, :].bitcast(FP8X4),
+                            lhsT_scale=x_scales[b][:, i, g, :],
                             rhs=w_codes[:, g, lo:hi].bitcast(FP8X4),
                             rhs_scale=w_scales[:, g, lo:hi],
                             start=(g == 0),
@@ -165,16 +163,15 @@ def tile_qwen3attention_pa_t_kernel(
                 )
             mean_sq_of[b] = mean_sq
 
-        def roots(b):
-            std = stat_pool.tile([P, BUNCH * QK_HEADS], F32, name="std")
-            nc.scalar.activation(
-                out=std[:], in_=mean_sq_of[b][:], func=ACT.Sqrt, bias=eps_col[:], scale=1.0
-            )
-            std_of[b] = std
-
-        def reciprocals(b):
+        def norm_factors(b):
             rstd = stat_pool.tile([P, BUNCH * QK_HEADS], F32, name="rstd")
-            nc.vector.reciprocal(rstd[:], std_of[b][:])
+            nc.scalar.activation(
+                out=rstd[:],
+                in_=mean_sq_of[b][:],
+                func=ACT.Abs_reciprocal_sqrt,
+                bias=eps_col[:],
+                scale=1.0,
+            )
             rstd_of[b] = rstd
 
         def copy_v(b):
@@ -188,42 +185,50 @@ def tile_qwen3attention_pa_t_kernel(
             c = b // BUNCHES_PER_CHUNK
             i0 = (b % BUNCHES_PER_CHUNK) * BUNCH
             rope = rope_of[c % CHUNKS_PER_BATCH]
-            if i0 == 0:
-                prods_of[c] = prod_pool.tile([P, 2, CHUNK, 2, 2, HEAD], F32, name="prods")
+            prods = prod_pool.tile([P, 2, BUNCH, 2, 2, HEAD], F32, name="prods")
             for i in range(BUNCH):
                 for qk in range(2):
                     for h in range(2):
                         n = i * QK_HEADS + qk * 2 + h
                         nc.vector.scalar_tensor_tensor(
-                            out=prods_of[c][:, qk, i0 + i, h, :, :],
+                            out=prods[:, qk, i, h, :, :],
                             in0=qk_sums[b][:, n, :].unsqueeze(1).broadcast_to([P, 2, HEAD]),
                             scalar=rstd_of[b][:, n : n + 1],
                             in1=rope[:, i0 + i, qk, :, :],
                             op0=ALU.mult,
                             op1=ALU.mult,
                         )
+            prods_of[b] = prods
 
-        def add_and_store(c):
-            qk_out = stage_pool.tile([P, 2, CHUNK, 2 * HEAD], F32, name="qk_out")
-            done = qk_out[:].rearrange("p q i (h d) -> p (q i h) d", d=HEAD)
-            terms = prods_of[c][:].rearrange("p q i h a d -> p (q i h) a d")
-            nc.gpsimd.tensor_tensor(
-                out=done[:, :, 0:HALF],
-                in0=terms[:, :, 0, 0:HALF],
-                in1=terms[:, :, 1, HALF:HEAD],
+        def add_halves(b):
+            c = b // BUNCHES_PER_CHUNK
+            i0 = (b % BUNCHES_PER_CHUNK) * BUNCH
+            if i0 == 0:
+                qk_stage[c] = stage_pool.tile([P, 2, CHUNK, 2 * HEAD], F32, name="qk_out")
+            done = qk_stage[c][:, :, i0 : i0 + BUNCH, :].rearrange(
+                "p q i (h d) -> p q (i h) d", d=HEAD
+            )
+            terms = prods_of[b][:].rearrange("p q i h a d -> p q (i h) a d")
+            adder = nc.vector if b == N_BUNCHES - 1 else nc.gpsimd
+            adder.tensor_tensor(
+                out=done[:, :, :, 0:HALF],
+                in0=terms[:, :, :, 0, 0:HALF],
+                in1=terms[:, :, :, 1, HALF:HEAD],
                 op=ALU.subtract,
             )
-            nc.gpsimd.tensor_tensor(
-                out=done[:, :, HALF:HEAD],
-                in0=terms[:, :, 0, HALF:HEAD],
-                in1=terms[:, :, 1, 0:HALF],
+            adder.tensor_tensor(
+                out=done[:, :, :, HALF:HEAD],
+                in0=terms[:, :, :, 0, HALF:HEAD],
+                in1=terms[:, :, :, 1, 0:HALF],
                 op=ALU.add,
             )
+
+        def store_chunk(c):
             batch = c // CHUNKS_PER_BATCH
             t0 = (c % CHUNKS_PER_BATCH) * CHUNK
             nc.sync.dma_start(out=v_rows[batch, :, t0 : t0 + CHUNK, :], in_=v_stage[c][:])
-            nc.sync.dma_start(out=q_rows[batch, :, t0 : t0 + CHUNK, :], in_=qk_out[:, 0])
-            nc.sync.dma_start(out=k_rows[batch, :, t0 : t0 + CHUNK, :], in_=qk_out[:, 1])
+            nc.sync.dma_start(out=q_rows[batch, :, t0 : t0 + CHUNK, :], in_=qk_stage[c][:, 0])
+            nc.sync.dma_start(out=k_rows[batch, :, t0 : t0 + CHUNK, :], in_=qk_stage[c][:, 1])
 
         w_sb = const.tile([P, OUT_COLS // P, FEAT], BF16, name="w_sb")
         gains = const.tile([P, 2, HEAD], BF16, name="gains")
@@ -231,11 +236,12 @@ def tile_qwen3attention_pa_t_kernel(
         sin_sb = const.tile([P, TILES_PER_BATCH, HEAD], BF16, name="sin_sb")
         load_bunch(0)
         nc.sync.dma_start(out=w_sb[:], in_=w_qkv.rearrange("(c p) k -> p c k", p=P))
+        load_bunch(1)
         nc.sync.dma_start(out=gains[:, 0, :], in_=q_norm_w.partition_broadcast(P))
         nc.sync.dma_start(out=gains[:, 1, :], in_=k_norm_w.partition_broadcast(P))
         nc.sync.dma_start(out=cos_sb[:], in_=cos_rows)
         nc.sync.dma_start(out=sin_sb[:], in_=sin_rows)
-        for b in range(1, X_BUFS):
+        for b in range(2, X_BUFS):
             load_bunch(b)
 
         ident = const.tile([P, P], F32, name="ident")
@@ -243,20 +249,19 @@ def tile_qwen3attention_pa_t_kernel(
         eps_col = const.tile([P, 1], F32, name="eps_col")
         nc.vector.memset(eps_col[:], EPS)
         warm = const.tile([P, 1], F32, name="warm")
-        nc.scalar.activation(out=warm[:], in_=eps_col[:], func=ACT.Sqrt)
+        nc.scalar.activation(out=warm[:], in_=eps_col[:], func=ACT.Abs_reciprocal_sqrt)
 
         for c in range(CHUNKS_PER_BATCH):
-            maker = nc.vector if c == 0 else nc.gpsimd
             tiles = slice(c * CHUNK, (c + 1) * CHUNK)
             rope_c = const.tile([P, CHUNK, 2, 2, HEAD], F32, name="rope%d" % c)
-            maker.tensor_tensor(
+            nc.gpsimd.tensor_tensor(
                 out=rope_c[:, :, :, 0, :],
                 in0=cos_sb[:, tiles, :].unsqueeze(2).broadcast_to([P, CHUNK, 2, HEAD]),
                 in1=gains[:].unsqueeze(1).broadcast_to([P, CHUNK, 2, HEAD]),
                 op=ALU.mult,
             )
             for mine, other in ((0, HALF), (HALF, 0)):
-                maker.tensor_tensor(
+                nc.gpsimd.tensor_tensor(
                     out=rope_c[:, :, :, 1, mine : mine + HALF],
                     in0=sin_sb[:, tiles, other : other + HALF]
                     .unsqueeze(2)
@@ -292,20 +297,19 @@ def tile_qwen3attention_pa_t_kernel(
             turn_bunch(b)
             for i in range(BUNCH):
                 regroup_tile(b * BUNCH + i)
-        quantise_chunk(0)
+        for b in range(QUANT_AHEAD):
+            quantise(b)
         for b in range(N_BUNCHES):
             ahead = b + TURN_AHEAD
-            c = b // BUNCHES_PER_CHUNK
             turn_bunch(ahead)
             project(b)
             regroup_tile(ahead * BUNCH)
             mean_squares(b)
             regroup_tile(ahead * BUNCH + 1)
-            roots(b)
-            if b % BUNCHES_PER_CHUNK == 0:
-                quantise_chunk(c + 1)
-            reciprocals(b)
+            norm_factors(b)
+            quantise(b + QUANT_AHEAD)
             copy_v(b)
             rope_products(b)
+            add_halves(b)
             if b % BUNCHES_PER_CHUNK == BUNCHES_PER_CHUNK - 1:
-                add_and_store(c)
+                store_chunk(b // BUNCHES_PER_CHUNK)

@@ -132,6 +132,8 @@ def tile_qwen3attention_pa_t_kernel(
             x_scales[b] = scales
 
         def project(b):
+            if b >= N_BUNCHES:
+                return
             qk_ps = psum_qk.tile([P, BUNCH, QK_COLS], F32, name="qk_ps")
             v_ps = psum_v.tile([P, BUNCH, V_COLS], F32, name="v_ps")
             for i in range(BUNCH):
@@ -150,6 +152,8 @@ def tile_qwen3attention_pa_t_kernel(
             v_sums[b] = v_ps
 
         def mean_squares(b):
+            if b >= N_BUNCHES:
+                return
             n_heads = BUNCH * QK_HEADS
             squares = stat_pool.tile([P, n_heads, HEAD], F32, name="squares")
             mean_sq = stat_pool.tile([P, n_heads], F32, name="mean_sq")
@@ -164,6 +168,8 @@ def tile_qwen3attention_pa_t_kernel(
             mean_sq_of[b] = mean_sq
 
         def norm_factors(b):
+            if b < 0:
+                return
             rstd = stat_pool.tile([P, BUNCH * QK_HEADS], F32, name="rstd")
             nc.scalar.activation(
                 out=rstd[:],
@@ -175,6 +181,8 @@ def tile_qwen3attention_pa_t_kernel(
             rstd_of[b] = rstd
 
         def copy_v(b):
+            if b >= N_BUNCHES:
+                return
             c = b // BUNCHES_PER_CHUNK
             i0 = (b % BUNCHES_PER_CHUNK) * BUNCH
             if i0 == 0:
@@ -182,6 +190,8 @@ def tile_qwen3attention_pa_t_kernel(
             nc.vector.tensor_copy(out=v_stage[c][:, i0 : i0 + BUNCH, :], in_=v_sums[b][:])
 
         def rope_products(b):
+            if b < 0:
+                return
             c = b // BUNCHES_PER_CHUNK
             i0 = (b % BUNCHES_PER_CHUNK) * BUNCH
             rope = rope_of[c % CHUNKS_PER_BATCH]
@@ -201,6 +211,8 @@ def tile_qwen3attention_pa_t_kernel(
             prods_of[b] = prods
 
         def add_halves(b):
+            if b < 0:
+                return
             c = b // BUNCHES_PER_CHUNK
             i0 = (b % BUNCHES_PER_CHUNK) * BUNCH
             if i0 == 0:
@@ -224,6 +236,8 @@ def tile_qwen3attention_pa_t_kernel(
             )
 
         def store_chunk(c):
+            if c < 0:
+                return
             batch = c // CHUNKS_PER_BATCH
             t0 = (c % CHUNKS_PER_BATCH) * CHUNK
             nc.sync.dma_start(out=v_rows[batch, :, t0 : t0 + CHUNK, :], in_=v_stage[c][:])
@@ -299,17 +313,17 @@ def tile_qwen3attention_pa_t_kernel(
                 regroup_tile(b * BUNCH + i)
         for b in range(QUANT_AHEAD):
             quantise(b)
-        for b in range(N_BUNCHES):
+        for b in range(N_BUNCHES + 1):
             ahead = b + TURN_AHEAD
             turn_bunch(ahead)
             project(b)
             regroup_tile(ahead * BUNCH)
-            mean_squares(b)
+            norm_factors(b - 1)
             regroup_tile(ahead * BUNCH + 1)
-            norm_factors(b)
+            mean_squares(b)
             quantise(b + QUANT_AHEAD)
             copy_v(b)
-            rope_products(b)
-            add_halves(b)
-            if b % BUNCHES_PER_CHUNK == BUNCHES_PER_CHUNK - 1:
-                store_chunk(b // BUNCHES_PER_CHUNK)
+            rope_products(b - 1)
+            add_halves(b - 1)
+            if b % BUNCHES_PER_CHUNK == 0:
+                store_chunk(b // BUNCHES_PER_CHUNK - 1)

@@ -187,7 +187,10 @@ def tile_qwen3attention_pa_t_kernel(
             i0 = (b % BUNCHES_PER_CHUNK) * BUNCH
             if i0 == 0:
                 v_stage[c] = stage_pool.tile([P, CHUNK, V_COLS], F32, name="v_out")
-            nc.vector.tensor_copy(out=v_stage[c][:, i0 : i0 + BUNCH, :], in_=v_sums[b][:])
+            if b % 2 == 0:
+                nc.vector.tensor_copy(out=v_stage[c][:, i0 : i0 + BUNCH, :], in_=v_sums[b][:])
+            else:
+                nc.scalar.copy(out=v_stage[c][:, i0 : i0 + BUNCH, :], in_=v_sums[b][:])
 
         def rope_products(b):
             if b < 0:

@@ -221,20 +221,14 @@ def tile_qwen3attention_pa_t_kernel(
             if i0 == 0:
                 qk_stage[c] = stage_pool.tile([P, 2, CHUNK, 2 * HEAD], F32, name="qk_out")
             done = qk_stage[c][:, :, i0 : i0 + BUNCH, :].rearrange(
-                "p q i (h d) -> p q (i h) d", d=HEAD
+                "p q i (h s d) -> p q (i h) s d", s=2, d=HALF
             )
-            terms = prods_of[b][:].rearrange("p q i h a d -> p q (i h) a d")
+            terms = prods_of[b][:].rearrange("p q i h a (s d) -> p q (i h) a s d", s=2)
             adder = nc.vector if b == N_BUNCHES - 1 else nc.gpsimd
             adder.tensor_tensor(
-                out=done[:, :, :, 0:HALF],
-                in0=terms[:, :, :, 0, 0:HALF],
-                in1=terms[:, :, :, 1, HALF:HEAD],
-                op=ALU.subtract,
-            )
-            adder.tensor_tensor(
-                out=done[:, :, :, HALF:HEAD],
-                in0=terms[:, :, :, 0, HALF:HEAD],
-                in1=terms[:, :, :, 1, 0:HALF],
+                out=done,
+                in0=terms[:, :, :, 0, :, :],
+                in1=terms[:, :, :, 1, ::-1, :],
                 op=ALU.add,
             )
 
@@ -268,6 +262,15 @@ def tile_qwen3attention_pa_t_kernel(
         warm = const.tile([P, 1], F32, name="warm")
         nc.scalar.activation(out=warm[:], in_=eps_col[:], func=ACT.Abs_reciprocal_sqrt)
 
+        signed_gains = const.tile([P, 2, HEAD], BF16, name="signed_gains")
+        nc.gpsimd.tensor_copy(out=signed_gains[:, :, 0:HALF], in_=gains[:, :, 0:HALF])
+        nc.gpsimd.tensor_scalar(
+            out=signed_gains[:, :, HALF:HEAD],
+            in0=gains[:, :, HALF:HEAD],
+            scalar1=-1.0,
+            scalar2=None,
+            op0=ALU.mult,
+        )
         for c in range(CHUNKS_PER_BATCH):
             tiles = slice(c * CHUNK, (c + 1) * CHUNK)
             rope_c = const.tile([P, CHUNK, 2, 2, HEAD], F32, name="rope%d" % c)
@@ -283,7 +286,7 @@ def tile_qwen3attention_pa_t_kernel(
                     in0=sin_sb[:, tiles, other : other + HALF]
                     .unsqueeze(2)
                     .broadcast_to([P, CHUNK, 2, HALF]),
-                    in1=gains[:, :, mine : mine + HALF]
+                    in1=signed_gains[:, :, mine : mine + HALF]
                     .unsqueeze(1)
                     .broadcast_to([P, CHUNK, 2, HALF]),
                     op=ALU.mult,

@@ -38,7 +38,8 @@ BUNCHES_PER_BATCH = TILES_PER_BATCH // BUNCH
 N_BUNCHES = BATCH * BUNCHES_PER_BATCH
 TURN_AHEAD = 3
 QUANT_AHEAD = 2
-X_BUFS = 12
+N_CHUNKS = BATCH * CHUNKS_PER_BATCH
+X_BUFS = 6
 assert BUNCH == 2
 
 FLOPS = 2 * BATCH * SEQ * FEAT * OUT_COLS
@@ -48,12 +49,12 @@ def tile_qwen3attention_pa_t_kernel(
     tc, x, pos_cos, pos_sin, w_qkv, q_norm_w, k_norm_w, out_0, out_1, out_2
 ):
     nc = tc.nc
-    x_rows = x.rearrange("b (p t) k -> b p t k", t=TILES_PER_BATCH)
-    cos_rows = pos_cos.rearrange("(p t) d -> p t d", t=TILES_PER_BATCH)
-    sin_rows = pos_sin.rearrange("(p t) d -> p t d", t=TILES_PER_BATCH)
-    q_rows = out_0.rearrange("b (p t) h d -> b p t (h d)", t=TILES_PER_BATCH)
-    k_rows = out_1.rearrange("b (p t) h d -> b p t (h d)", t=TILES_PER_BATCH)
-    v_rows = out_2.rearrange("b (p t) h d -> b p t (h d)", t=TILES_PER_BATCH)
+    x_rows = x.rearrange("b (c p i) k -> b c p i k", p=P, i=CHUNK)
+    cos_rows = pos_cos.rearrange("(c p i) d -> p c i d", p=P, i=CHUNK)
+    sin_rows = pos_sin.rearrange("(c p i) d -> p c i d", p=P, i=CHUNK)
+    q_rows = out_0.rearrange("b (c p i) h d -> b c p i (h d)", p=P, i=CHUNK)
+    k_rows = out_1.rearrange("b (c p i) h d -> b c p i (h d)", p=P, i=CHUNK)
+    v_rows = out_2.rearrange("b (c p i) h d -> b c p i (h d)", p=P, i=CHUNK)
 
     with ExitStack() as ctx:
         const = ctx.enter_context(tc.tile_pool(name="const", bufs=1))
@@ -82,15 +83,17 @@ def tile_qwen3attention_pa_t_kernel(
         qk_stage = {}
         v_stage = {}
 
-        def load_bunch(b):
-            if b >= N_BUNCHES:
+        def load_chunk(c):
+            if c >= N_CHUNKS:
                 return
-            t0 = (b % BUNCHES_PER_BATCH) * BUNCH
-            x_sb = x_pool.tile([P, BUNCH, FEAT], BF16, name="x_sb")
+            x_sb = x_pool.tile([P, CHUNK, FEAT], BF16, name="x_sb")
             nc.sync.dma_start(
-                out=x_sb[:], in_=x_rows[b // BUNCHES_PER_BATCH, :, t0 : t0 + BUNCH, :]
+                out=x_sb[:], in_=x_rows[c // CHUNKS_PER_BATCH, c % CHUNKS_PER_BATCH]
             )
-            x_words[b] = x_sb[:].bitcast(F32)
+            for j in range(BUNCHES_PER_CHUNK):
+                x_words[c * BUNCHES_PER_CHUNK + j] = x_sb[
+                    :, j * BUNCH : (j + 1) * BUNCH, :
+                ].bitcast(F32)
 
         def turn_rows(words):
             turned = psum_t.tile([P, WORD_BLOCKS, P], F32, name="turned")
@@ -103,7 +106,8 @@ def tile_qwen3attention_pa_t_kernel(
                 return
             for i in range(BUNCH):
                 turned_of[b * BUNCH + i] = turn_rows(x_words[b][:, i, :])
-            load_bunch(b + X_BUFS)
+            if b % BUNCHES_PER_CHUNK == BUNCHES_PER_CHUNK - 1:
+                load_chunk(b // BUNCHES_PER_CHUNK + X_BUFS)
 
         def regroup_tile(tile):
             if tile >= N_BUNCHES * BUNCH:
@@ -236,24 +240,31 @@ def tile_qwen3attention_pa_t_kernel(
             if c < 0:
                 return
             batch = c // CHUNKS_PER_BATCH
-            t0 = (c % CHUNKS_PER_BATCH) * CHUNK
-            nc.sync.dma_start(out=v_rows[batch, :, t0 : t0 + CHUNK, :], in_=v_stage[c][:])
-            nc.sync.dma_start(out=q_rows[batch, :, t0 : t0 + CHUNK, :], in_=qk_stage[c][:, 0])
-            nc.sync.dma_start(out=k_rows[batch, :, t0 : t0 + CHUNK, :], in_=qk_stage[c][:, 1])
+            part = c % CHUNKS_PER_BATCH
+            nc.sync.dma_start(out=v_rows[batch, part], in_=v_stage[c][:])
+            nc.sync.dma_start(out=q_rows[batch, part], in_=qk_stage[c][:, 0])
+            nc.sync.dma_start(out=k_rows[batch, part], in_=qk_stage[c][:, 1])
 
         w_sb = const.tile([P, OUT_COLS // P, FEAT], BF16, name="w_sb")
         gains = const.tile([P, 2, HEAD], BF16, name="gains")
         cos_sb = const.tile([P, TILES_PER_BATCH, HEAD], BF16, name="cos_sb")
         sin_sb = const.tile([P, TILES_PER_BATCH, HEAD], BF16, name="sin_sb")
-        load_bunch(0)
+        x_first = x_pool.tile([P, CHUNK, FEAT], BF16, name="x_sb")
+        for j in range(BUNCHES_PER_CHUNK):
+            x_words[j] = x_first[:, j * BUNCH : (j + 1) * BUNCH, :].bitcast(F32)
+        nc.sync.dma_start(out=x_first[:, 0:BUNCH, :], in_=x_rows[0, 0, :, 0:BUNCH, :])
         nc.sync.dma_start(out=w_sb[:], in_=w_qkv.rearrange("(c p) k -> p c k", p=P))
-        load_bunch(1)
+        nc.sync.dma_start(out=x_first[:, BUNCH:CHUNK, :], in_=x_rows[0, 0, :, BUNCH:CHUNK, :])
         nc.sync.dma_start(out=gains[:, 0, :], in_=q_norm_w.partition_broadcast(P))
         nc.sync.dma_start(out=gains[:, 1, :], in_=k_norm_w.partition_broadcast(P))
-        nc.sync.dma_start(out=cos_sb[:], in_=cos_rows)
-        nc.sync.dma_start(out=sin_sb[:], in_=sin_rows)
-        for b in range(2, X_BUFS):
-            load_bunch(b)
+        nc.sync.dma_start(
+            out=cos_sb[:].rearrange("p (c i) d -> p c i d", i=CHUNK), in_=cos_rows
+        )
+        nc.sync.dma_start(
+            out=sin_sb[:].rearrange("p (c i) d -> p c i d", i=CHUNK), in_=sin_rows
+        )
+        for c in range(1, X_BUFS):
+            load_chunk(c)
 
         ident = const.tile([P, P], F32, name="ident")
         make_identity(nc, ident[:])

@@ -245,18 +245,21 @@ def tile_qwen3attention_pa_t_kernel(
             nc.sync.dma_start(out=q_rows[batch, part], in_=qk_stage[c][:, 0])
             nc.sync.dma_start(out=k_rows[batch, part], in_=qk_stage[c][:, 1])
 
+        gain_rows = const.tile([P, 2, HEAD], BF16, name="gain_rows")
+        nc.vector.memset(gain_rows[:], 0.0)
+        ones = const.tile([P, P], BF16, name="ones")
+        nc.vector.memset(ones[:], 1.0)
         w_sb = const.tile([P, OUT_COLS // P, FEAT], BF16, name="w_sb")
-        gains = const.tile([P, 2, HEAD], BF16, name="gains")
         cos_sb = const.tile([P, TILES_PER_BATCH, HEAD], BF16, name="cos_sb")
         sin_sb = const.tile([P, TILES_PER_BATCH, HEAD], BF16, name="sin_sb")
         x_first = x_pool.tile([P, CHUNK, FEAT], BF16, name="x_sb")
         for j in range(BUNCHES_PER_CHUNK):
             x_words[j] = x_first[:, j * BUNCH : (j + 1) * BUNCH, :].bitcast(F32)
         nc.sync.dma_start(out=x_first[:, 0:BUNCH, :], in_=x_rows[0, 0, :, 0:BUNCH, :])
+        nc.sync.dma_start(out=gain_rows[0:1, 0, :], in_=q_norm_w.rearrange("(o d) -> o d", o=1))
+        nc.sync.dma_start(out=gain_rows[0:1, 1, :], in_=k_norm_w.rearrange("(o d) -> o d", o=1))
         nc.sync.dma_start(out=w_sb[:], in_=w_qkv.rearrange("(c p) k -> p c k", p=P))
         nc.sync.dma_start(out=x_first[:, BUNCH:CHUNK, :], in_=x_rows[0, 0, :, BUNCH:CHUNK, :])
-        nc.sync.dma_start(out=gains[:, 0, :], in_=q_norm_w.partition_broadcast(P))
-        nc.sync.dma_start(out=gains[:, 1, :], in_=k_norm_w.partition_broadcast(P))
         nc.sync.dma_start(
             out=cos_sb[:].rearrange("p (c i) d -> p c i d", i=CHUNK), in_=cos_rows
         )
@@ -273,6 +276,22 @@ def tile_qwen3attention_pa_t_kernel(
         warm = const.tile([P, 1], F32, name="warm")
         nc.scalar.activation(out=warm[:], in_=eps_col[:], func=ACT.Abs_reciprocal_sqrt)
 
+        turn_bunch(0)
+        for i in range(BUNCH):
+            regroup_tile(i)
+
+        spread = psum_t.tile([P, WORD_BLOCKS, P], F32, name="turned")
+        nc.tensor.matmul(
+            out=spread[:, 0, :],
+            lhsT=ones[:],
+            rhs=gain_rows[:].rearrange("p q d -> p (q d)"),
+            start=True,
+            stop=True,
+        )
+        gains = const.tile([P, 2, HEAD], BF16, name="gains")
+        nc.vector.tensor_copy(
+            out=gains[:].rearrange("p q d -> p (q d)"), in_=spread[:, 0, :]
+        )
         signed_gains = const.tile([P, 2, HEAD], BF16, name="signed_gains")
         nc.gpsimd.tensor_copy(out=signed_gains[:, :, 0:HALF], in_=gains[:, :, 0:HALF])
         nc.gpsimd.tensor_scalar(
@@ -303,10 +322,6 @@ def tile_qwen3attention_pa_t_kernel(
                     op=ALU.mult,
                 )
             rope_of[c] = rope_c
-
-        turn_bunch(0)
-        for i in range(BUNCH):
-            regroup_tile(i)
 
         w_words = w_sb[:].bitcast(F32)
         w_grouped = const.tile([P, PASSES, OUT_COLS * PACK], BF16, name="w_grouped", align_bytes=64)

@@ -83,13 +83,17 @@ def tile_qwen3attention_pa_t_kernel(
         qk_stage = {}
         v_stage = {}
 
-        def load_chunk(c):
+        def load_chunk(c, pieces=(CHUNK,)):
             if c >= N_CHUNKS:
                 return
             x_sb = x_pool.tile([P, CHUNK, FEAT], BF16, name="x_sb")
-            nc.sync.dma_start(
-                out=x_sb[:], in_=x_rows[c // CHUNKS_PER_BATCH, c % CHUNKS_PER_BATCH]
-            )
+            rows = x_rows[c // CHUNKS_PER_BATCH, c % CHUNKS_PER_BATCH]
+            first = 0
+            for count in pieces:
+                nc.sync.dma_start(
+                    out=x_sb[:, first : first + count, :], in_=rows[:, first : first + count, :]
+                )
+                first += count
             for j in range(BUNCHES_PER_CHUNK):
                 x_words[c * BUNCHES_PER_CHUNK + j] = x_sb[
                     :, j * BUNCH : (j + 1) * BUNCH, :
@@ -236,14 +240,13 @@ def tile_qwen3attention_pa_t_kernel(
                 op=ALU.add,
             )
 
-        def store_chunk(c):
-            if c < 0:
-                return
+        def store_tiles(c, first, count):
             batch = c // CHUNKS_PER_BATCH
             part = c % CHUNKS_PER_BATCH
-            nc.sync.dma_start(out=v_rows[batch, part], in_=v_stage[c][:])
-            nc.sync.dma_start(out=q_rows[batch, part], in_=qk_stage[c][:, 0])
-            nc.sync.dma_start(out=k_rows[batch, part], in_=qk_stage[c][:, 1])
+            tiles = slice(first, first + count)
+            nc.sync.dma_start(out=v_rows[batch, part, :, tiles, :], in_=v_stage[c][:, tiles, :])
+            nc.sync.dma_start(out=q_rows[batch, part, :, tiles, :], in_=qk_stage[c][:, 0, tiles, :])
+            nc.sync.dma_start(out=k_rows[batch, part, :, tiles, :], in_=qk_stage[c][:, 1, tiles, :])
 
         gain_rows = const.tile([P, 2, HEAD], BF16, name="gain_rows")
         nc.vector.memset(gain_rows[:], 0.0)
@@ -255,18 +258,22 @@ def tile_qwen3attention_pa_t_kernel(
         x_first = x_pool.tile([P, CHUNK, FEAT], BF16, name="x_sb")
         for j in range(BUNCHES_PER_CHUNK):
             x_words[j] = x_first[:, j * BUNCH : (j + 1) * BUNCH, :].bitcast(F32)
-        nc.sync.dma_start(out=x_first[:, 0:BUNCH, :], in_=x_rows[0, 0, :, 0:BUNCH, :])
+        for i in range(BUNCH):
+            nc.sync.dma_start(out=x_first[:, i : i + 1, :], in_=x_rows[0, 0, :, i : i + 1, :])
         nc.sync.dma_start(out=gain_rows[0:1, 0, :], in_=q_norm_w.rearrange("(o d) -> o d", o=1))
         nc.sync.dma_start(out=gain_rows[0:1, 1, :], in_=k_norm_w.rearrange("(o d) -> o d", o=1))
-        nc.sync.dma_start(out=w_sb[:], in_=w_qkv.rearrange("(c p) k -> p c k", p=P))
+        for blk in range(OUT_COLS // P):
+            nc.sync.dma_start(out=w_sb[:, blk, :], in_=w_qkv[blk * P : (blk + 1) * P, :])
+        cos_chunks = cos_sb[:].rearrange("p (c i) d -> p c i d", i=CHUNK)
+        sin_chunks = sin_sb[:].rearrange("p (c i) d -> p c i d", i=CHUNK)
+        nc.sync.dma_start(out=cos_chunks[:, 0:1], in_=cos_rows[:, 0:1])
+        nc.sync.dma_start(out=sin_chunks[:, 0:1], in_=sin_rows[:, 0:1])
         nc.sync.dma_start(out=x_first[:, BUNCH:CHUNK, :], in_=x_rows[0, 0, :, BUNCH:CHUNK, :])
-        nc.sync.dma_start(
-            out=cos_sb[:].rearrange("p (c i) d -> p c i d", i=CHUNK), in_=cos_rows
-        )
-        nc.sync.dma_start(
-            out=sin_sb[:].rearrange("p (c i) d -> p c i d", i=CHUNK), in_=sin_rows
-        )
-        for c in range(1, X_BUFS):
+        load_chunk(1, (BUNCH, BUNCH))
+        load_chunk(2)
+        nc.sync.dma_start(out=cos_chunks[:, 1:], in_=cos_rows[:, 1:])
+        nc.sync.dma_start(out=sin_chunks[:, 1:], in_=sin_rows[:, 1:])
+        for c in range(3, X_BUFS):
             load_chunk(c)
 
         ident = const.tile([P, P], F32, name="ident")
@@ -301,7 +308,10 @@ def tile_qwen3attention_pa_t_kernel(
             scalar2=None,
             op0=ALU.mult,
         )
-        for c in range(CHUNKS_PER_BATCH):
+
+        def rope_factors(c):
+            if c >= CHUNKS_PER_BATCH:
+                return
             tiles = slice(c * CHUNK, (c + 1) * CHUNK)
             rope_c = const.tile([P, CHUNK, 2, 2, HEAD], F32, name="rope%d" % c)
             nc.gpsimd.tensor_tensor(
@@ -322,6 +332,9 @@ def tile_qwen3attention_pa_t_kernel(
                     op=ALU.mult,
                 )
             rope_of[c] = rope_c
+
+        rope_factors(0)
+        rope_factors(1)
 
         w_words = w_sb[:].bitcast(F32)
         w_grouped = const.tile([P, PASSES, OUT_COLS * PACK], BF16, name="w_grouped", align_bytes=64)
@@ -354,8 +367,13 @@ def tile_qwen3attention_pa_t_kernel(
             regroup_tile(ahead * BUNCH + 1)
             mean_squares(b)
             quantise(b + QUANT_AHEAD)
-            copy_v(b)
+            if b != N_BUNCHES - 1:
+                copy_v(min(b, N_BUNCHES - 1))
             rope_products(b - 1)
             add_halves(b - 1)
-            if b % BUNCHES_PER_CHUNK == 0:
-                store_chunk(b // BUNCHES_PER_CHUNK - 1)
+            if b % BUNCHES_PER_CHUNK == 1:
+                rope_factors(b // BUNCHES_PER_CHUNK + 2)
+            if b % BUNCHES_PER_CHUNK == 0 and 0 < b < N_BUNCHES:
+                store_tiles(b // BUNCHES_PER_CHUNK - 1, 0, CHUNK)
+            if b >= N_BUNCHES - 1:
+                store_tiles(N_CHUNKS - 1, (b - N_BUNCHES + 1) * BUNCH, BUNCH)

from contextlib import ExitStack

import concourse.mybir as mybir
from concourse.masks import make_identity

F32 = mybir.dt.float32
BF16 = mybir.dt.bfloat16
U32 = mybir.dt.uint32
U8 = mybir.dt.uint8
FP8X4 = mybir.dt.float8_e4m3fn_x4
ACT = mybir.ActivationFunctionType
ALU = mybir.AluOpType

P = 128
BATCH = 4
SEQ = 2048
FEAT = 1024
HEAD = 64
HALF = HEAD // 2
QK_HEADS = 4
QK_COLS = QK_HEADS * HEAD
OUT_COLS = 384
V_COLS = OUT_COLS - QK_COLS
EPS = 1e-6

PACK = 4
PASSES = FEAT // (P * PACK)
PAIR = 2
WORDS = FEAT // PAIR
WORD_BLOCKS = WORDS // P

TILES_PER_BATCH = SEQ // P
BUNCH = 2
CHUNK = 4
BUNCHES_PER_CHUNK = CHUNK // BUNCH
CHUNKS_PER_BATCH = TILES_PER_BATCH // CHUNK
BUNCHES_PER_BATCH = TILES_PER_BATCH // BUNCH
N_BUNCHES = BATCH * BUNCHES_PER_BATCH
TURN_AHEAD = 3
QUANT_AHEAD = 2
N_CHUNKS = BATCH * CHUNKS_PER_BATCH
X_BUFS = 6
assert BUNCH == 2

FLOPS = 2 * BATCH * SEQ * FEAT * OUT_COLS


def tile_qwen3attention_pa_t_kernel(
    tc, x, pos_cos, pos_sin, w_qkv, q_norm_w, k_norm_w, out_0, out_1, out_2
):
    nc = tc.nc
    x_rows = x.rearrange("b (c p i) k -> b c p i k", p=P, i=CHUNK)
    cos_rows = pos_cos.rearrange("(c p i) d -> p c i d", p=P, i=CHUNK)
    sin_rows = pos_sin.rearrange("(c p i) d -> p c i d", p=P, i=CHUNK)
    q_rows = out_0.rearrange("b (c p i) h d -> b c p i (h d)", p=P, i=CHUNK)
    k_rows = out_1.rearrange("b (c p i) h d -> b c p i (h d)", p=P, i=CHUNK)
    v_rows = out_2.rearrange("b (c p i) h d -> b c p i (h d)", p=P, i=CHUNK)

    with ExitStack() as ctx:
        const = ctx.enter_context(tc.tile_pool(name="const", bufs=1))
        x_pool = ctx.enter_context(tc.tile_pool(name="x_pool", bufs=X_BUFS))
        group_pool = ctx.enter_context(tc.tile_pool(name="group_pool", bufs=3))
        code_pool = ctx.enter_context(tc.tile_pool(name="code_pool", bufs=QUANT_AHEAD + 2))
        stat_pool = ctx.enter_context(tc.tile_pool(name="stat_pool", bufs=3))
        prod_pool = ctx.enter_context(tc.tile_pool(name="prod_pool", bufs=3))
        stage_pool = ctx.enter_context(tc.tile_pool(name="stage_pool", bufs=4))
        psum_t = ctx.enter_context(tc.psum_pool(name="psum_t", bufs=3))
        psum_qk = ctx.enter_context(tc.psum_pool(name="psum_qk", bufs=3))
        psum_v = ctx.enter_context(tc.psum_pool(name="psum_v", bufs=2))
        ctx.enter_context(tc.manual_schedule())

        x_words = {}
        turned_of = {}
        grouped_of = {}
        x_codes = {}
        x_scales = {}
        qk_sums = {}
        v_sums = {}
        mean_sq_of = {}
        rstd_of = {}
        rope_of = {}
        prods_of = {}
        qk_stage = {}
        v_stage = {}

        def load_chunk(c, pieces=(CHUNK,)):
            if c >= N_CHUNKS:
                return
            x_sb = x_pool.tile([P, CHUNK, FEAT], BF16, name="x_sb")
            rows = x_rows[c // CHUNKS_PER_BATCH, c % CHUNKS_PER_BATCH]
            first = 0
            for count in pieces:
                nc.sync.dma_start(
                    out=x_sb[:, first : first + count, :], in_=rows[:, first : first + count, :]
                )
                first += count
            for j in range(BUNCHES_PER_CHUNK):
                x_words[c * BUNCHES_PER_CHUNK + j] = x_sb[
                    :, j * BUNCH : (j + 1) * BUNCH, :
                ].bitcast(F32)

        def turn_rows(words):
            turned = psum_t.tile([P, WORD_BLOCKS, P], F32, name="turned")
            for j in range(WORD_BLOCKS):
                nc.tensor.transpose(turned[:, j, :], words[:, j * P : (j + 1) * P], ident[:])
            return turned[:].rearrange("p (g u) r -> p g r u", u=PAIR)

        def turn_bunch(b):
            if b >= N_BUNCHES:
                return
            for i in range(BUNCH):
                turned_of[b * BUNCH + i] = turn_rows(x_words[b][:, i, :])
            if b % BUNCHES_PER_CHUNK == BUNCHES_PER_CHUNK - 1:
                load_chunk(b // BUNCHES_PER_CHUNK + X_BUFS)

        def regroup_tile(tile):
            if tile >= N_BUNCHES * BUNCH:
                return
            b = tile // BUNCH
            if tile % BUNCH == 0:
                grouped_of[b] = group_pool.tile(
                    [P, BUNCH, PASSES, P * PACK], BF16, name="grouped", align_bytes=64
                )
            grouped_words = grouped_of[b][:].bitcast(F32).rearrange(
                "p i g (r u) -> p i g r u", u=PAIR
            )
            nc.scalar.copy(out=grouped_words[:, tile % BUNCH], in_=turned_of[tile])

        def quantise(b):
            if b >= N_BUNCHES:
                return
            codes = code_pool.tile([P, BUNCH, PASSES, P], U32, name="codes", align_bytes=64)
            scales = code_pool.tile([P, BUNCH, PASSES, P], U8, name="scales", align_bytes=64)
            nc.vector.quantize_mx(
                out=codes[:].rearrange("p i g r -> p (i g r)").bitcast(FP8X4),
                scales=scales[:].rearrange("p i g r -> p (i g r)"),
                in_=grouped_of[b][:].rearrange("p i g c -> p (i g c)"),
            )
            x_codes[b] = codes
            x_scales[b] = scales

        def project(b):
            if b >= N_BUNCHES:
                return
            qk_ps = psum_qk.tile([P, BUNCH, QK_COLS], F32, name="qk_ps")
            v_ps = psum_v.tile([P, BUNCH, V_COLS], F32, name="v_ps")
            for i in range(BUNCH):
                for g in range(PASSES):
                    for acc, lo, hi in ((qk_ps, 0, QK_COLS), (v_ps, QK_COLS, OUT_COLS)):
                        nc.tensor.matmul_mx(
                            out=acc[:, i, :],
                            lhsT=x_codes[b][:, i, g, :].bitcast(FP8X4),
                            lhsT_scale=x_scales[b][:, i, g, :],
                            rhs=w_codes[:, g, lo:hi].bitcast(FP8X4),
                            rhs_scale=w_scales[:, g, lo:hi],
                            start=(g == 0),
                            stop=(g == PASSES - 1),
                        )
            qk_sums[b] = qk_ps[:].rearrange("p i (h d) -> p (i h) d", d=HEAD)
            v_sums[b] = v_ps

        def mean_squares(b):
            if b >= N_BUNCHES:
                return
            n_heads = BUNCH * QK_HEADS
            squares = stat_pool.tile([P, n_heads, HEAD], F32, name="squares")
            mean_sq = stat_pool.tile([P, n_heads], F32, name="mean_sq")
            for n in range(n_heads):
                nc.scalar.activation(
                    out=squares[:, n, :],
                    in_=qk_sums[b][:, n, :],
                    func=ACT.Square,
                    scale=1.0 / 8.0,
                    accum_out=mean_sq[:, n : n + 1],
                )
            mean_sq_of[b] = mean_sq

        def norm_factors(b):
            if b < 0:
                return
            rstd = stat_pool.tile([P, BUNCH * QK_HEADS], F32, name="rstd")
            nc.scalar.activation(
                out=rstd[:],
                in_=mean_sq_of[b][:],
                func=ACT.Abs_reciprocal_sqrt,
                bias=eps_col[:],
                scale=1.0,
            )
            rstd_of[b] = rstd

        def copy_v(b):
            if b >= N_BUNCHES:
                return
            c = b // BUNCHES_PER_CHUNK
            i0 = (b % BUNCHES_PER_CHUNK) * BUNCH
            if i0 == 0:
                v_stage[c] = stage_pool.tile([P, CHUNK, V_COLS], F32, name="v_out")
            if b % 2 == 0:
                nc.vector.tensor_copy(out=v_stage[c][:, i0 : i0 + BUNCH, :], in_=v_sums[b][:])
            else:
                nc.scalar.copy(out=v_stage[c][:, i0 : i0 + BUNCH, :], in_=v_sums[b][:])

        def rope_products(b):
            if b < 0:
                return
            c = b // BUNCHES_PER_CHUNK
            i0 = (b % BUNCHES_PER_CHUNK) * BUNCH
            rope = rope_of[c % CHUNKS_PER_BATCH]
            prods = prod_pool.tile([P, 2, BUNCH, 2, 2, HEAD], F32, name="prods")
            for i in range(BUNCH):
                for qk in range(2):
                    for h in range(2):
                        n = i * QK_HEADS + qk * 2 + h
                        nc.vector.scalar_tensor_tensor(
                            out=prods[:, qk, i, h, :, :],
                            in0=qk_sums[b][:, n, :].unsqueeze(1).broadcast_to([P, 2, HEAD]),
                            scalar=rstd_of[b][:, n : n + 1],
                            in1=rope[:, i0 + i, qk, :, :],
                            op0=ALU.mult,
                            op1=ALU.mult,
                        )
            prods_of[b] = prods

        def add_halves(b):
            if b < 0:
                return
            c = b // BUNCHES_PER_CHUNK
            i0 = (b % BUNCHES_PER_CHUNK) * BUNCH
            if i0 == 0:
                qk_stage[c] = stage_pool.tile([P, 2, CHUNK, 2 * HEAD], F32, name="qk_out")
            done = qk_stage[c][:, :, i0 : i0 + BUNCH, :].rearrange(
                "p q i (h s d) -> p q (i h) s d", s=2, d=HALF
            )
            terms = prods_of[b][:].rearrange("p q i h a (s d) -> p q (i h) a s d", s=2)
            adder = nc.vector if b == N_BUNCHES - 1 else nc.gpsimd
            adder.tensor_tensor(
                out=done,
                in0=terms[:, :, :, 0, :, :],
                in1=terms[:, :, :, 1, ::-1, :],
                op=ALU.add,
            )

        def store_tiles(c, first, count):
            batch = c // CHUNKS_PER_BATCH
            part = c % CHUNKS_PER_BATCH
            tiles = slice(first, first + count)
            nc.sync.dma_start(out=v_rows[batch, part, :, tiles, :], in_=v_stage[c][:, tiles, :])
            nc.sync.dma_start(out=q_rows[batch, part, :, tiles, :], in_=qk_stage[c][:, 0, tiles, :])
            nc.sync.dma_start(out=k_rows[batch, part, :, tiles, :], in_=qk_stage[c][:, 1, tiles, :])

        gain_rows = const.tile([P, 2, HEAD], BF16, name="gain_rows")
        nc.vector.memset(gain_rows[:], 0.0)
        ones = const.tile([P, P], BF16, name="ones")
        nc.vector.memset(ones[:], 1.0)
        w_sb = const.tile([P, OUT_COLS // P, FEAT], BF16, name="w_sb")
        cos_sb = const.tile([P, TILES_PER_BATCH, HEAD], BF16, name="cos_sb")
        sin_sb = const.tile([P, TILES_PER_BATCH, HEAD], BF16, name="sin_sb")
        x_first = x_pool.tile([P, CHUNK, FEAT], BF16, name="x_sb")
        for j in range(BUNCHES_PER_CHUNK):
            x_words[j] = x_first[:, j * BUNCH : (j + 1) * BUNCH, :].bitcast(F32)
        for i in range(BUNCH):
            nc.sync.dma_start(out=x_first[:, i : i + 1, :], in_=x_rows[0, 0, :, i : i + 1, :])
        nc.sync.dma_start(out=gain_rows[0:1, 0, :], in_=q_norm_w.rearrange("(o d) -> o d", o=1))
        nc.sync.dma_start(out=gain_rows[0:1, 1, :], in_=k_norm_w.rearrange("(o d) -> o d", o=1))
        for blk in range(OUT_COLS // P):
            nc.sync.dma_start(out=w_sb[:, blk, :], in_=w_qkv[blk * P : (blk + 1) * P, :])
        cos_chunks = cos_sb[:].rearrange("p (c i) d -> p c i d", i=CHUNK)
        sin_chunks = sin_sb[:].rearrange("p (c i) d -> p c i d", i=CHUNK)
        nc.sync.dma_start(out=cos_chunks[:, 0:1], in_=cos_rows[:, 0:1])
        nc.sync.dma_start(out=sin_chunks[:, 0:1], in_=sin_rows[:, 0:1])
        nc.sync.dma_start(out=x_first[:, BUNCH:CHUNK, :], in_=x_rows[0, 0, :, BUNCH:CHUNK, :])
        load_chunk(1, (BUNCH, BUNCH))
        load_chunk(2)
        nc.sync.dma_start(out=cos_chunks[:, 1:], in_=cos_rows[:, 1:])
        nc.sync.dma_start(out=sin_chunks[:, 1:], in_=sin_rows[:, 1:])
        for c in range(3, X_BUFS):
            load_chunk(c)

        ident = const.tile([P, P], F32, name="ident")
        make_identity(nc, ident[:])
        eps_col = const.tile([P, 1], F32, name="eps_col")
        nc.vector.memset(eps_col[:], EPS)
        warm = const.tile([P, 1], F32, name="warm")
        nc.scalar.activation(out=warm[:], in_=eps_col[:], func=ACT.Abs_reciprocal_sqrt)

        turn_bunch(0)
        for i in range(BUNCH):
            regroup_tile(i)

        spread = psum_t.tile([P, WORD_BLOCKS, P], F32, name="turned")
        nc.tensor.matmul(
            out=spread[:, 0, :],
            lhsT=ones[:],
            rhs=gain_rows[:].rearrange("p q d -> p (q d)"),
            start=True,
            stop=True,
        )
        gains = const.tile([P, 2, HEAD], BF16, name="gains")
        nc.vector.tensor_copy(
            out=gains[:].rearrange("p q d -> p (q d)"), in_=spread[:, 0, :]
        )
        signed_gains = const.tile([P, 2, HEAD], BF16, name="signed_gains")
        nc.gpsimd.tensor_copy(out=signed_gains[:, :, 0:HALF], in_=gains[:, :, 0:HALF])
        nc.gpsimd.tensor_scalar(
            out=signed_gains[:, :, HALF:HEAD],
            in0=gains[:, :, HALF:HEAD],
            scalar1=-1.0,
            scalar2=None,
            op0=ALU.mult,
        )

        def rope_factors(c):
            if c >= CHUNKS_PER_BATCH:
                return
            tiles = slice(c * CHUNK, (c + 1) * CHUNK)
            rope_c = const.tile([P, CHUNK, 2, 2, HEAD], F32, name="rope%d" % c)
            nc.gpsimd.tensor_tensor(
                out=rope_c[:, :, :, 0, :],
                in0=cos_sb[:, tiles, :].unsqueeze(2).broadcast_to([P, CHUNK, 2, HEAD]),
                in1=gains[:].unsqueeze(1).broadcast_to([P, CHUNK, 2, HEAD]),
                op=ALU.mult,
            )
            for mine, other in ((0, HALF), (HALF, 0)):
                nc.gpsimd.tensor_tensor(
                    out=rope_c[:, :, :, 1, mine : mine + HALF],
                    in0=sin_sb[:, tiles, other : other + HALF]
                    .unsqueeze(2)
                    .broadcast_to([P, CHUNK, 2, HALF]),
                    in1=signed_gains[:, :, mine : mine + HALF]
                    .unsqueeze(1)
                    .broadcast_to([P, CHUNK, 2, HALF]),
                    op=ALU.mult,
                )
            rope_of[c] = rope_c

        rope_factors(0)
        rope_factors(1)

        w_words = w_sb[:].bitcast(F32)
        w_grouped = const.tile([P, PASSES, OUT_COLS * PACK], BF16, name="w_grouped", align_bytes=64)
        w_grouped_words = w_grouped[:].bitcast(F32).rearrange("p g (e u) -> p g e u", u=PAIR)
        w_codes = const.tile([P, PASSES, OUT_COLS], U32, name="w_codes", align_bytes=64)
        w_scales = const.tile([P, PASSES, OUT_COLS], U8, name="w_scales", align_bytes=64)
        for blk in range(OUT_COLS // P):
            turned_w = turn_rows(w_words[:, blk, :])
            nc.scalar.copy(out=w_grouped_words[:, :, blk * P : (blk + 1) * P, :], in_=turned_w)
        for g in range(PASSES):
            for lo, hi in ((0, QK_COLS), (QK_COLS, OUT_COLS)):
                nc.vector.quantize_mx(
                    out=w_codes[:, g, lo:hi].bitcast(FP8X4),
                    scales=w_scales[:, g, lo:hi],
                    in_=w_grouped[:, g, lo * PACK : hi * PACK],
                )

        for b in range(1, TURN_AHEAD):
            turn_bunch(b)
            for i in range(BUNCH):
                regroup_tile(b * BUNCH + i)
        for b in range(QUANT_AHEAD):
            quantise(b)
        for b in range(N_BUNCHES + 1):
            ahead = b + TURN_AHEAD
            turn_bunch(ahead)
            project(b)
            regroup_tile(ahead * BUNCH)
            norm_factors(b - 1)
            regroup_tile(ahead * BUNCH + 1)
            mean_squares(b)
            quantise(b + QUANT_AHEAD)
            if b != N_BUNCHES - 1:
                copy_v(min(b, N_BUNCHES - 1))
            rope_products(b - 1)
            add_halves(b - 1)
            if b % BUNCHES_PER_CHUNK == 1:
                rope_factors(b // BUNCHES_PER_CHUNK + 2)
            if b % BUNCHES_PER_CHUNK == 0 and 0 < b < N_BUNCHES:
                store_tiles(b // BUNCHES_PER_CHUNK - 1, 0, CHUNK)
            if b >= N_BUNCHES - 1:
                store_tiles(N_CHUNKS - 1, (b - N_BUNCHES + 1) * BUNCH, BUNCH)
